import numpy as np
import ml_dtypes


def mxq(x, axis, fmt="e4m3"):
    dtype, down = {"e4m3": (ml_dtypes.float8_e4m3fn, 7), "e5m2": (ml_dtypes.float8_e5m2, 14)}[fmt]
    v = np.moveaxis(np.asarray(x, np.float32).astype(ml_dtypes.bfloat16).astype(np.float64), axis, -1)
    blocks = v.reshape(v.shape[:-1] + (-1, 32))
    amax = np.abs(blocks).max(-1, keepdims=True)
    byte = np.maximum(np.where(amax > 0, np.frexp(amax)[1] - 1 + 127, 0) - down, 1)
    scale = np.exp2(byte - 127.0)
    codes = (blocks / scale).astype(np.float32).astype(dtype).astype(np.float64)
    return np.moveaxis((codes * scale).reshape(v.shape), -1, axis)


WIDE = False


def mx_kscale(k):
    if not WIDE:
        return np.ones(k)
    levels = np.array([10, -10, 5, -5, 0])
    a = np.random.permutation(np.resize(levels, k // 512 * 4)).reshape(k // 512, 4)
    idx = np.arange(k)
    return np.exp2(a[idx // 512, idx % 128 // 32])


BF16 = ml_dtypes.bfloat16


def bf(x):
    return np.asarray(x, np.float32).astype(BF16)


def f64(x):
    return np.asarray(x).astype(np.float64)


R, C, E, H = 4, 512, 512, 4
D = E // H
RD = R * D


def setup_inputs():
    s = mx_kscale(E)
    return {"attn_weights": bf(np.random.standard_normal((H, C, C)) * 2.0),
            "mask0": bf(np.random.uniform(size=C) < 0.1),
            "x": bf(np.random.standard_normal((R, C, E)) * s),
            "Wv": bf(np.random.standard_normal((E, E)) * 2.0 / np.sqrt(E) / s[:, None]),
            "bv": bf(np.random.standard_normal(E) * 0.1)}


def reference(attn_weights, mask0, x, Wv, bv):
    m0 = f64(mask0)[None, :, None]
    a = f64(attn_weights) * (1.0 - m0) + m0 * (-10000.0)
    e = np.exp(a - a.max(-1, keepdims=True))
    p = e / e.sum(-1, keepdims=True)
    v = (mxq(f64(x), 2, "e4m3") @ mxq(f64(Wv), 0, "e4m3")) + f64(bv)
    vm = v.reshape(R, C, H, D).transpose(2, 1, 0, 3).reshape(H, C, RD)
    ctx = mxq(p, 2, "e4m3") @ mxq(vm, 1, "e4m3")
    return ctx.reshape(H, C, R, D).transpose(2, 1, 0, 3).reshape(R, C, E)

@@ -1,0 +1,250 @@
+from contextlib import ExitStack
+
+import concourse.mybir as mybir
+from concourse.masks import make_identity
+
+F32 = mybir.dt.float32
+BF16 = mybir.dt.bfloat16
+U32 = mybir.dt.uint32
+U8 = mybir.dt.uint8
+FP8X4 = mybir.dt.float8_e4m3fn_x4
+ALU = mybir.AluOpType
+ACT = mybir.ActivationFunctionType
+AXIS = mybir.AxisListType
+
+P = 128
+PACK = 4
+R, C, E, H = 4, 512, 512, 4
+D = E // H
+TILES = C // P
+MASKED_LOGIT = -10000.0
+
+FLOPS = 2 * R * C * E * E + 2 * H * C * C * R * D
+
+
+def tile_rowselfattention_pb_kernel(tc, attn_weights, mask0, x, Wv, bv, out):
+    nc = tc.nc
+    with ExitStack() as ctx:
+        keep_pool = ctx.enter_context(tc.tile_pool(name="keep", bufs=1))
+        work = ctx.enter_context(tc.tile_pool(name="work", bufs=2))
+        stores = ctx.enter_context(tc.tile_pool(name="stores", bufs=6))
+        psum = ctx.enter_context(tc.psum_pool(name="psum", bufs=2))
+
+        bias_row = keep_pool.tile([P, E], BF16, name="bias_row")
+        nc.vector.memset(bias_row[:], 0.0)
+        nc.scalar.dma_start(out=bias_row[0:1, :], in_=bv.rearrange("(o e) -> o e", o=1))
+        mask_rows = keep_pool.tile([P, P], BF16, name="mask_rows")
+        nc.vector.memset(mask_rows[:], 0.0)
+        nc.scalar.dma_start(out=mask_rows[0:TILES, :], in_=mask0.rearrange("(t p) -> t p", p=P))
+
+        w_raw = keep_pool.tile([P, PACK, E], BF16, name="w_raw")
+        nc.sync.dma_start(
+            out=w_raw[:].rearrange("q (u e) c -> q u e c", u=2),
+            in_=Wv.rearrange("(u q e) c -> q u e c", u=2, e=2),
+        )
+        x_sb = []
+        a_sb = []
+        for r in range(R):
+            x_sb.append(keep_pool.tile([P, TILES, E], BF16, name="x_sb%d" % r))
+            a_sb.append(keep_pool.tile([P, H, C], BF16, name="a_sb%d" % r))
+        for r in range(R):
+            nc.sync.dma_start(out=x_sb[r][:], in_=x[r].rearrange("(t p) k -> p t k", p=P))
+        for it in range(TILES):
+            nc.sync.dma_start(
+                out=a_sb[it][:],
+                in_=attn_weights[:, it * P : (it + 1) * P, :].rearrange("h p j -> p h j"),
+            )
+
+        warm_in = keep_pool.tile([P, 1], F32, name="warm_in")
+        warm_out = keep_pool.tile([P, 1], F32, name="warm_out")
+        nc.vector.memset(warm_in[:], 0.0)
+        nc.scalar.activation(out=warm_out[:], in_=warm_in[:], func=ACT.Exp)
+
+        ident_f32 = keep_pool.tile([P, P], F32, name="ident_f32")
+        make_identity(nc, ident_f32[:])
+        ident_bf = keep_pool.tile([P, P], BF16, name="ident_bf")
+        make_identity(nc, ident_bf[:])
+        ones = keep_pool.tile([P, P], BF16, name="ones")
+        nc.vector.memset(ones[:], 1.0)
+
+        bias_ps = psum.tile([P, E], F32, tag="xt")
+        nc.tensor.matmul(out=bias_ps[:], lhsT=ones[:], rhs=bias_row[:], start=True, stop=True)
+        bias_bc = keep_pool.tile([P, E], F32, name="bias_bc")
+        nc.vector.tensor_copy(out=bias_bc[:], in_=bias_ps[:])
+
+        mask_ps = psum.tile([P, P], BF16, tag="pt")
+        nc.tensor.transpose(mask_ps[:], mask_rows[:], ident_bf[:])
+        mask_col = keep_pool.tile([P, TILES], F32, name="mask_col")
+        nc.vector.tensor_copy(out=mask_col[:], in_=mask_ps[:, 0:TILES])
+        keep = keep_pool.tile([P, TILES], F32, name="keep")
+        nc.vector.tensor_scalar(
+            out=keep[:], in0=mask_col[:], scalar1=-1.0, scalar2=1.0, op0=ALU.mult, op1=ALU.add
+        )
+        fill = keep_pool.tile([P, TILES], F32, name="fill")
+        nc.vector.tensor_scalar(
+            out=fill[:], in0=mask_col[:], scalar1=MASKED_LOGIT, scalar2=None, op0=ALU.mult
+        )
+
+        w_grouped = keep_pool.tile([P, E, PACK], BF16, name="w_grouped", align_bytes=64)
+        nc.vector.tensor_copy(out=w_grouped[:], in_=w_raw[:].rearrange("q t c -> q c t"))
+        w_codes = keep_pool.tile([P, E], U32, name="w_codes", align_bytes=64)
+        w_scales = keep_pool.tile([P, E], U8, name="w_scales", align_bytes=64)
+        nc.vector.quantize_mx(
+            out=w_codes[:].bitcast(FP8X4),
+            scales=w_scales[:],
+            in_=w_grouped[:].rearrange("q c t -> q (c t)"),
+        )
+
+        x_codes = []
+        x_scales = []
+        v_codes = []
+        v_scales = []
+        p_codes = []
+        p_scales = []
+        for n in range(R):
+            x_codes.append(keep_pool.tile([P, C], U32, name="x_codes%d" % n, align_bytes=64))
+            x_scales.append(keep_pool.tile([P, C], U8, name="x_scales%d" % n, align_bytes=64))
+            v_codes.append(keep_pool.tile([P, E], U32, name="v_codes%d" % n, align_bytes=64))
+            v_scales.append(keep_pool.tile([P, E], U8, name="v_scales%d" % n, align_bytes=64))
+            p_codes.append(keep_pool.tile([P, H * P], U32, name="p_codes%d" % n, align_bytes=64))
+            p_scales.append(keep_pool.tile([P, H * P], U8, name="p_scales%d" % n, align_bytes=64))
+
+        def x_to_codes(r):
+            x_grouped = work.tile([P, C, PACK], BF16, name="x_grouped", align_bytes=64)
+            grouped_words = (
+                x_grouped[:].rearrange("p j t -> p (j t)").bitcast(F32)
+                .rearrange("p (g j u) -> p g j u", g=TILES, u=2)
+            )
+            for half in range(2):
+                xt_ps = psum.tile([P, 2, 2, P], F32, tag="xt")
+                for g in range(2):
+                    words = x_sb[r][:, 2 * half + g, :].bitcast(F32)
+                    for u in range(2):
+                        nc.tensor.transpose(
+                            xt_ps[:, g, u, :], words[:, u * P : (u + 1) * P], ident_f32[:]
+                        )
+                nc.scalar.copy(
+                    out=grouped_words[:, 2 * half : 2 * half + 2, :, :],
+                    in_=xt_ps[:].rearrange("p g u j -> p g j u"),
+                )
+            nc.vector.quantize_mx(
+                out=x_codes[r][:].bitcast(FP8X4),
+                scales=x_scales[r][:],
+                in_=x_grouped[:].rearrange("p j t -> p (j t)"),
+            )
+
+        def project(r):
+            v_grouped = work.tile([P, H, D, PACK], BF16, name="v_grouped", align_bytes=64)
+            for h in range(H):
+                v_ps = psum.tile([P, PACK, D], F32, tag="v")
+                for t in range(PACK):
+                    nc.tensor.matmul_mx(
+                        out=v_ps[:, t, :],
+                        lhsT=x_codes[r][:, t * P : (t + 1) * P].bitcast(FP8X4),
+                        lhsT_scale=x_scales[r][:, t * P : (t + 1) * P],
+                        rhs=w_codes[:, h * D : (h + 1) * D].bitcast(FP8X4),
+                        rhs_scale=w_scales[:, h * D : (h + 1) * D],
+                        start=True,
+                        stop=True,
+                    )
+                nc.vector.tensor_tensor(
+                    out=v_grouped[:, h, :, :],
+                    in0=v_ps[:].rearrange("p t d -> p d t"),
+                    in1=bias_bc[:, h * D : (h + 1) * D].unsqueeze(2).to_broadcast([P, D, PACK]),
+                    op=ALU.add,
+                )
+            nc.vector.quantize_mx(
+                out=v_codes[r][:].bitcast(FP8X4),
+                scales=v_scales[r][:],
+                in_=v_grouped[:].rearrange("p h d t -> p (h d t)"),
+            )
+
+        def softmax(it):
+            a = a_sb[it]
+            half_a = work.tile([P, H, C // 2], BF16, name="half_a")
+            nc.vector.tensor_tensor(
+                out=half_a[:], in0=a[:, :, 0 : C // 2], in1=a[:, :, C // 2 : C], op=ALU.max
+            )
+            half_b = work.tile([P, H, C // 4], BF16, name="half_b")
+            nc.vector.tensor_tensor(
+                out=half_b[:], in0=half_a[:, :, 0 : C // 4], in1=half_a[:, :, C // 4 : C // 2],
+                op=ALU.max,
+            )
+            half_c = work.tile([P, H, C // 8], BF16, name="half_c")
+            nc.vector.tensor_tensor(
+                out=half_c[:], in0=half_b[:, :, 0 : C // 8], in1=half_b[:, :, C // 8 : C // 4],
+                op=ALU.max,
+            )
+            row_max = work.tile([P, H], F32, name="row_max")
+            nc.vector.tensor_reduce(out=row_max[:], in_=half_c[:], axis=AXIS.X, op=ALU.max)
+            masked_max = work.tile([P, H], F32, name="masked_max")
+            nc.vector.tensor_scalar(
+                out=masked_max[:], in0=row_max[:], scalar1=keep[:, it : it + 1],
+                scalar2=fill[:, it : it + 1], op0=ALU.mult, op1=ALU.add,
+            )
+            shift = work.tile([P, H], F32, name="shift")
+            nc.vector.tensor_tensor(
+                out=shift[:], in0=fill[:, it : it + 1].to_broadcast([P, H]), in1=masked_max[:],
+                op=ALU.subtract,
+            )
+            e = work.tile([P, H, C], F32, name="e")
+            row_sum = work.tile([P, H], F32, name="row_sum")
+            for h in range(H):
+                nc.scalar.activation(
+                    out=e[:, h, :], in_=a[:, h, :], func=ACT.Exp, bias=shift[:, h : h + 1],
+                    scale=keep[:, it : it + 1], accum_out=row_sum[:, h : h + 1],
+                )
+            inv_sum = work.tile([P, H], F32, name="inv_sum")
+            nc.vector.reciprocal(out=inv_sum[:], in_=row_sum[:])
+            p_bf = work.tile([P, H, C], BF16, name="p_bf")
+            for h in range(H):
+                nc.vector.tensor_scalar(
+                    out=p_bf[:, h, :], in0=e[:, h, :], scalar1=inv_sum[:, h : h + 1], scalar2=None,
+                    op0=ALU.mult,
+                )
+            return p_bf
+
+        def p_to_codes(it, p_bf):
+            p_grouped = work.tile([P, H, P, PACK], BF16, name="p_grouped", align_bytes=64)
+            for h in range(H):
+                pt_ps = psum.tile([P, PACK, P], BF16, tag="pt")
+                for t in range(PACK):
+                    nc.tensor.transpose(
+                        pt_ps[:, t, :], p_bf[:, h, t * P : (t + 1) * P], ident_bf[:]
+                    )
+                nc.scalar.copy(
+                    out=p_grouped[:, h, :, :], in_=pt_ps[:].rearrange("p t i -> p i t")
+                )
+            nc.vector.quantize_mx(
+                out=p_codes[it][:].bitcast(FP8X4),
+                scales=p_scales[it][:],
+                in_=p_grouped[:].rearrange("p h i t -> p (h i t)"),
+            )
+
+        def attend(it, r):
+            o_ps = psum.tile([P, H, D], F32, tag="o")
+            for h in range(H):
+                nc.tensor.matmul_mx(
+                    out=o_ps[:, h, :],
+                    lhsT=p_codes[it][:, h * P : (h + 1) * P].bitcast(FP8X4),
+                    lhsT_scale=p_scales[it][:, h * P : (h + 1) * P],
+                    rhs=v_codes[r][:, h * D : (h + 1) * D].bitcast(FP8X4),
+                    rhs_scale=v_scales[r][:, h * D : (h + 1) * D],
+                    start=True,
+                    stop=True,
+                )
+            o_sb = stores.tile([P, E], F32, name="o_sb")
+            if r == R - 1:
+                nc.vector.tensor_copy(out=o_sb[:], in_=o_ps[:].rearrange("p h d -> p (h d)"))
+            else:
+                nc.scalar.copy(out=o_sb[:], in_=o_ps[:].rearrange("p h d -> p (h d)"))
+            nc.sync.dma_start(out=out[r, it * P : (it + 1) * P, :], in_=o_sb[:])
+
+        for r in range(R):
+            x_to_codes(r)
+            project(r)
+        for it in range(TILES):
+            p_bf = softmax(it)
+            p_to_codes(it, p_bf)
+            for r in range(R):
+                attend(it, r)

@@ -17,7 +17,6 @@ PACK = 4
 R, C, E, H = 4, 512, 512, 4
 D = E // H
 TILES = C // P
-MASKED_LOGIT = -10000.0
 
 FLOPS = 2 * R * C * E * E + 2 * H * C * C * R * D
 
@@ -27,73 +26,85 @@ def tile_rowselfattention_pb_kernel(tc, attn_weights, mask0, x, Wv, bv, out):
     with ExitStack() as ctx:
         keep_pool = ctx.enter_context(tc.tile_pool(name="keep", bufs=1))
         work = ctx.enter_context(tc.tile_pool(name="work", bufs=2))
+        stats = ctx.enter_context(tc.tile_pool(name="stats", bufs=8))
         stores = ctx.enter_context(tc.tile_pool(name="stores", bufs=6))
-        psum = ctx.enter_context(tc.psum_pool(name="psum", bufs=2))
+        psum = ctx.enter_context(tc.psum_pool(name="psum", bufs=8))
 
+        mask_col = keep_pool.tile([P, TILES], BF16, name="mask_col")
         bias_row = keep_pool.tile([P, E], BF16, name="bias_row")
-        nc.vector.memset(bias_row[:], 0.0)
-        nc.scalar.dma_start(out=bias_row[0:1, :], in_=bv.rearrange("(o e) -> o e", o=1))
-        mask_rows = keep_pool.tile([P, P], BF16, name="mask_rows")
-        nc.vector.memset(mask_rows[:], 0.0)
-        nc.scalar.dma_start(out=mask_rows[0:TILES, :], in_=mask0.rearrange("(t p) -> t p", p=P))
-
+        nc.gpsimd.memset(bias_row[:], 0.0)
         w_raw = keep_pool.tile([P, PACK, E], BF16, name="w_raw")
+        x_sb = []
+        a_sb = []
+        for n in range(R):
+            x_sb.append(keep_pool.tile([P, TILES, E], BF16, name="x_sb%d" % n))
+            a_sb.append(keep_pool.tile([P, H, C], BF16, name="a_sb%d" % n))
+
+        def pieces(it):
+            step = 1 if it == 0 else H
+            return [(h0, h0 + step) for h0 in range(0, H, step)]
+
+        def load_logits(it):
+            for h0, h1 in pieces(it):
+                nc.sync.dma_start(
+                    out=a_sb[it][:, h0:h1, :],
+                    in_=attn_weights[h0:h1, it * P : (it + 1) * P, :].rearrange("h p j -> p h j"),
+                )
+
+        def load_x(r):
+            nc.sync.dma_start(out=x_sb[r][:], in_=x[r].rearrange("(t p) k -> p t k", p=P))
+
+        with nc.allow_non_contiguous_dma(reason="512 mask values, one query column to a partition"):
+            nc.sync.dma_start(out=mask_col[:], in_=mask0.rearrange("(t p) -> p t", p=P))
+        load_logits(0)
+        load_logits(1)
         nc.sync.dma_start(
             out=w_raw[:].rearrange("q (u e) c -> q u e c", u=2),
             in_=Wv.rearrange("(u q e) c -> q u e c", u=2, e=2),
         )
-        x_sb = []
-        a_sb = []
-        for r in range(R):
-            x_sb.append(keep_pool.tile([P, TILES, E], BF16, name="x_sb%d" % r))
-            a_sb.append(keep_pool.tile([P, H, C], BF16, name="a_sb%d" % r))
-        for r in range(R):
-            nc.sync.dma_start(out=x_sb[r][:], in_=x[r].rearrange("(t p) k -> p t k", p=P))
-        for it in range(TILES):
-            nc.sync.dma_start(
-                out=a_sb[it][:],
-                in_=attn_weights[:, it * P : (it + 1) * P, :].rearrange("h p j -> p h j"),
-            )
+        nc.sync.dma_start(out=bias_row[0:1, :], in_=bv.rearrange("(o e) -> o e", o=1))
+        load_x(0)
+        load_x(1)
+        for n in range(2, R):
+            load_logits(n)
+            load_x(n)
 
         warm_in = keep_pool.tile([P, 1], F32, name="warm_in")
         warm_out = keep_pool.tile([P, 1], F32, name="warm_out")
         nc.vector.memset(warm_in[:], 0.0)
         nc.scalar.activation(out=warm_out[:], in_=warm_in[:], func=ACT.Exp)
 
-        ident_f32 = keep_pool.tile([P, P], F32, name="ident_f32")
-        make_identity(nc, ident_f32[:])
         ident_bf = keep_pool.tile([P, P], BF16, name="ident_bf")
         make_identity(nc, ident_bf[:])
+        ident_f32 = keep_pool.tile([P, P], F32, name="ident_f32")
+        make_identity(nc, ident_f32[:])
         ones = keep_pool.tile([P, P], BF16, name="ones")
         nc.vector.memset(ones[:], 1.0)
 
-        bias_ps = psum.tile([P, E], F32, tag="xt")
-        nc.tensor.matmul(out=bias_ps[:], lhsT=ones[:], rhs=bias_row[:], start=True, stop=True)
-        bias_bc = keep_pool.tile([P, E], F32, name="bias_bc")
-        nc.vector.tensor_copy(out=bias_bc[:], in_=bias_ps[:])
-
-        mask_ps = psum.tile([P, P], BF16, tag="pt")
-        nc.tensor.transpose(mask_ps[:], mask_rows[:], ident_bf[:])
-        mask_col = keep_pool.tile([P, TILES], F32, name="mask_col")
-        nc.vector.tensor_copy(out=mask_col[:], in_=mask_ps[:, 0:TILES])
         keep = keep_pool.tile([P, TILES], F32, name="keep")
         nc.vector.tensor_scalar(
             out=keep[:], in0=mask_col[:], scalar1=-1.0, scalar2=1.0, op0=ALU.mult, op1=ALU.add
         )
-        fill = keep_pool.tile([P, TILES], F32, name="fill")
+        neg_keep = keep_pool.tile([P, TILES], F32, name="neg_keep")
         nc.vector.tensor_scalar(
-            out=fill[:], in0=mask_col[:], scalar1=MASKED_LOGIT, scalar2=None, op0=ALU.mult
+            out=neg_keep[:], in0=mask_col[:], scalar1=-1.0, scalar2=None, op0=ALU.add
         )
 
-        w_grouped = keep_pool.tile([P, E, PACK], BF16, name="w_grouped", align_bytes=64)
-        nc.vector.tensor_copy(out=w_grouped[:], in_=w_raw[:].rearrange("q t c -> q c t"))
+        bias_bc = keep_pool.tile([P, E], F32, name="bias_bc")
         w_codes = keep_pool.tile([P, E], U32, name="w_codes", align_bytes=64)
         w_scales = keep_pool.tile([P, E], U8, name="w_scales", align_bytes=64)
-        nc.vector.quantize_mx(
-            out=w_codes[:].bitcast(FP8X4),
-            scales=w_scales[:],
-            in_=w_grouped[:].rearrange("q c t -> q (c t)"),
-        )
+
+        def prepare_weights():
+            bias_ps = psum.tile([P, E], F32, tag="bank")
+            nc.tensor.matmul(out=bias_ps[:], lhsT=ones[:], rhs=bias_row[:], start=True, stop=True)
+            nc.vector.tensor_copy(out=bias_bc[:], in_=bias_ps[:])
+            w_grouped = keep_pool.tile([P, E, PACK], BF16, name="w_grouped", align_bytes=64)
+            nc.vector.tensor_copy(out=w_grouped[:], in_=w_raw[:].rearrange("q t c -> q c t"))
+            nc.vector.quantize_mx(
+                out=w_codes[:].bitcast(FP8X4),
+                scales=w_scales[:],
+                in_=w_grouped[:].rearrange("q c t -> q (c t)"),
+            )
 
         x_codes = []
         x_scales = []
@@ -109,14 +120,22 @@ def tile_rowselfattention_pb_kernel(tc, attn_weights, mask0, x, Wv, bv, out):
             p_codes.append(keep_pool.tile([P, H * P], U32, name="p_codes%d" % n, align_bytes=64))
             p_scales.append(keep_pool.tile([P, H * P], U8, name="p_scales%d" % n, align_bytes=64))
 
-        def x_to_codes(r):
-            x_grouped = work.tile([P, C, PACK], BF16, name="x_grouped", align_bytes=64)
+        x_grouped = {}
+        v_grouped = {}
+        shift = {}
+        e = {}
+        row_sum = {}
+        p_bf = {}
+        p_grouped = {}
+
+        def transpose_x(r):
+            x_grouped[r] = work.tile([P, C, PACK], BF16, name="x_grouped", align_bytes=64)
             grouped_words = (
-                x_grouped[:].rearrange("p j t -> p (j t)").bitcast(F32)
+                x_grouped[r][:].rearrange("p j t -> p (j t)").bitcast(F32)
                 .rearrange("p (g j u) -> p g j u", g=TILES, u=2)
             )
             for half in range(2):
-                xt_ps = psum.tile([P, 2, 2, P], F32, tag="xt")
+                xt_ps = psum.tile([P, 2, 2, P], F32, tag="bank")
                 for g in range(2):
                     words = x_sb[r][:, 2 * half + g, :].bitcast(F32)
                     for u in range(2):
@@ -127,102 +146,110 @@ def tile_rowselfattention_pb_kernel(tc, attn_weights, mask0, x, Wv, bv, out):
                     out=grouped_words[:, 2 * half : 2 * half + 2, :, :],
                     in_=xt_ps[:].rearrange("p g u j -> p g j u"),
                 )
+
+        def quantise_x(r):
             nc.vector.quantize_mx(
                 out=x_codes[r][:].bitcast(FP8X4),
                 scales=x_scales[r][:],
-                in_=x_grouped[:].rearrange("p j t -> p (j t)"),
+                in_=x_grouped[r][:].rearrange("p j t -> p (j t)"),
             )
 
-        def project(r):
-            v_grouped = work.tile([P, H, D, PACK], BF16, name="v_grouped", align_bytes=64)
-            for h in range(H):
-                v_ps = psum.tile([P, PACK, D], F32, tag="v")
-                for t in range(PACK):
-                    nc.tensor.matmul_mx(
-                        out=v_ps[:, t, :],
-                        lhsT=x_codes[r][:, t * P : (t + 1) * P].bitcast(FP8X4),
-                        lhsT_scale=x_scales[r][:, t * P : (t + 1) * P],
-                        rhs=w_codes[:, h * D : (h + 1) * D].bitcast(FP8X4),
-                        rhs_scale=w_scales[:, h * D : (h + 1) * D],
-                        start=True,
-                        stop=True,
-                    )
-                nc.vector.tensor_tensor(
-                    out=v_grouped[:, h, :, :],
-                    in0=v_ps[:].rearrange("p t d -> p d t"),
-                    in1=bias_bc[:, h * D : (h + 1) * D].unsqueeze(2).to_broadcast([P, D, PACK]),
-                    op=ALU.add,
+        def project_head(r, h):
+            if h == 0:
+                v_grouped[r] = work.tile([P, H, D, PACK], BF16, name="v_grouped", align_bytes=64)
+            v_ps = psum.tile([P, PACK, D], F32, tag="bank")
+            for t in range(PACK):
+                nc.tensor.matmul_mx(
+                    out=v_ps[:, t, :],
+                    lhsT=x_codes[r][:, t * P : (t + 1) * P].bitcast(FP8X4),
+                    lhsT_scale=x_scales[r][:, t * P : (t + 1) * P],
+                    rhs=w_codes[:, h * D : (h + 1) * D].bitcast(FP8X4),
+                    rhs_scale=w_scales[:, h * D : (h + 1) * D],
+                    start=True,
+                    stop=True,
                 )
+            nc.vector.tensor_tensor(
+                out=v_grouped[r][:, h, :, :],
+                in0=v_ps[:].rearrange("p t d -> p d t"),
+                in1=bias_bc[:, h * D : (h + 1) * D].unsqueeze(2).to_broadcast([P, D, PACK]),
+                op=ALU.add,
+            )
+
+        def quantise_v(r):
             nc.vector.quantize_mx(
                 out=v_codes[r][:].bitcast(FP8X4),
                 scales=v_scales[r][:],
-                in_=v_grouped[:].rearrange("p h d t -> p (h d t)"),
+                in_=v_grouped[r][:].rearrange("p h d t -> p (h d t)"),
             )
 
-        def softmax(it):
-            a = a_sb[it]
-            half_a = work.tile([P, H, C // 2], BF16, name="half_a")
+        def row_max(it, h0, h1):
+            a = a_sb[it][:, h0:h1, :]
+            heads = h1 - h0
+            half_a = work.tile([P, heads, C // 2], BF16, name="half_a")
             nc.vector.tensor_tensor(
                 out=half_a[:], in0=a[:, :, 0 : C // 2], in1=a[:, :, C // 2 : C], op=ALU.max
             )
-            half_b = work.tile([P, H, C // 4], BF16, name="half_b")
+            half_b = work.tile([P, heads, C // 4], BF16, name="half_b")
             nc.vector.tensor_tensor(
                 out=half_b[:], in0=half_a[:, :, 0 : C // 4], in1=half_a[:, :, C // 4 : C // 2],
                 op=ALU.max,
             )
-            half_c = work.tile([P, H, C // 8], BF16, name="half_c")
+            half_c = work.tile([P, heads, C // 8], BF16, name="half_c")
             nc.vector.tensor_tensor(
                 out=half_c[:], in0=half_b[:, :, 0 : C // 8], in1=half_b[:, :, C // 8 : C // 4],
                 op=ALU.max,
             )
-            row_max = work.tile([P, H], F32, name="row_max")
-            nc.vector.tensor_reduce(out=row_max[:], in_=half_c[:], axis=AXIS.X, op=ALU.max)
-            masked_max = work.tile([P, H], F32, name="masked_max")
+            logit_max = stats.tile([P, heads], F32, name="logit_max")
+            nc.vector.tensor_reduce(out=logit_max[:], in_=half_c[:], axis=AXIS.X, op=ALU.max)
+            shifts = stats.tile([P, heads], F32, name="shifts")
             nc.vector.tensor_scalar(
-                out=masked_max[:], in0=row_max[:], scalar1=keep[:, it : it + 1],
-                scalar2=fill[:, it : it + 1], op0=ALU.mult, op1=ALU.add,
+                out=shifts[:], in0=logit_max[:], scalar1=neg_keep[:, it : it + 1], scalar2=None,
+                op0=ALU.mult,
             )
-            shift = work.tile([P, H], F32, name="shift")
-            nc.vector.tensor_tensor(
-                out=shift[:], in0=fill[:, it : it + 1].to_broadcast([P, H]), in1=masked_max[:],
-                op=ALU.subtract,
-            )
-            e = work.tile([P, H, C], F32, name="e")
-            row_sum = work.tile([P, H], F32, name="row_sum")
+            for h in range(h0, h1):
+                shift[(it, h)] = shifts[:, h - h0 : h - h0 + 1]
+
+        def exponentials(it):
+            e[it] = work.tile([P, H, C], F32, name="e")
+            row_sum[it] = stats.tile([P, H], F32, name="row_sum")
             for h in range(H):
                 nc.scalar.activation(
-                    out=e[:, h, :], in_=a[:, h, :], func=ACT.Exp, bias=shift[:, h : h + 1],
-                    scale=keep[:, it : it + 1], accum_out=row_sum[:, h : h + 1],
+                    out=e[it][:, h, :], in_=a_sb[it][:, h, :], func=ACT.Exp,
+                    bias=shift[(it, h)], scale=keep[:, it : it + 1],
+                    accum_out=row_sum[it][:, h : h + 1],
                 )
-            inv_sum = work.tile([P, H], F32, name="inv_sum")
-            nc.vector.reciprocal(out=inv_sum[:], in_=row_sum[:])
-            p_bf = work.tile([P, H, C], BF16, name="p_bf")
+
+        def normalise(it):
+            inv_sum = stats.tile([P, H], F32, name="inv_sum")
+            nc.vector.reciprocal(out=inv_sum[:], in_=row_sum[it][:])
+            p_bf[it] = work.tile([P, H, C], BF16, name="p_bf")
             for h in range(H):
                 nc.vector.tensor_scalar(
-                    out=p_bf[:, h, :], in0=e[:, h, :], scalar1=inv_sum[:, h : h + 1], scalar2=None,
-                    op0=ALU.mult,
+                    out=p_bf[it][:, h, :], in0=e[it][:, h, :], scalar1=inv_sum[:, h : h + 1],
+                    scalar2=None, op0=ALU.mult,
                 )
-            return p_bf
 
-        def p_to_codes(it, p_bf):
-            p_grouped = work.tile([P, H, P, PACK], BF16, name="p_grouped", align_bytes=64)
-            for h in range(H):
-                pt_ps = psum.tile([P, PACK, P], BF16, tag="pt")
-                for t in range(PACK):
-                    nc.tensor.transpose(
-                        pt_ps[:, t, :], p_bf[:, h, t * P : (t + 1) * P], ident_bf[:]
-                    )
-                nc.scalar.copy(
-                    out=p_grouped[:, h, :, :], in_=pt_ps[:].rearrange("p t i -> p i t")
+        def transpose_p_head(it, h):
+            if h == 0:
+                p_grouped[it] = work.tile([P, H, P, PACK], BF16, name="p_grouped", align_bytes=64)
+            pt_ps = psum.tile([P, PACK, P], BF16, tag="bank")
+            for t in range(PACK):
+                nc.tensor.transpose(
+                    pt_ps[:, t, :], p_bf[it][:, h, t * P : (t + 1) * P], ident_bf[:]
                 )
+            nc.scalar.copy(
+                out=p_grouped[it][:, h, :, :], in_=pt_ps[:].rearrange("p t i -> p i t")
+            )
+
+        def quantise_p(it):
             nc.vector.quantize_mx(
                 out=p_codes[it][:].bitcast(FP8X4),
                 scales=p_scales[it][:],
-                in_=p_grouped[:].rearrange("p h i t -> p (h i t)"),
+                in_=p_grouped[it][:].rearrange("p h i t -> p (h i t)"),
             )
 
         def attend(it, r):
-            o_ps = psum.tile([P, H, D], F32, tag="o")
+            o_ps = psum.tile([P, H, D], F32, tag="bank")
             for h in range(H):
                 nc.tensor.matmul_mx(
                     out=o_ps[:, h, :],
@@ -240,11 +267,33 @@ def tile_rowselfattention_pb_kernel(tc, attn_weights, mask0, x, Wv, bv, out):
                 nc.scalar.copy(out=o_sb[:], in_=o_ps[:].rearrange("p h d -> p (h d)"))
             nc.sync.dma_start(out=out[r, it * P : (it + 1) * P, :], in_=o_sb[:])
 
-        for r in range(R):
-            x_to_codes(r)
-            project(r)
-        for it in range(TILES):
-            p_bf = softmax(it)
-            p_to_codes(it, p_bf)
-            for r in range(R):
-                attend(it, r)
+        def valid(n):
+            return 0 <= n < TILES
+
+        for k in range(-2, TILES + 2):
+            if valid(k + 2):
+                for h0, h1 in pieces(k + 2):
+                    row_max(k + 2, h0, h1)
+            if k == -2:
+                prepare_weights()
+            if valid(k + 1):
+                exponentials(k + 1)
+            if valid(k):
+                quantise_x(k)
+            ready = [
+                (it, r) for it in range(TILES) for r in range(R) if max(it + 1, r + 2) == k
+            ]
+            for h in range(H):
+                if valid(k - 1):
+                    project_head(k - 1, h)
+                if valid(k):
+                    transpose_p_head(k, h)
+                for it, r in ready[h::H]:
+                    attend(it, r)
+            if valid(k + 1):
+                transpose_x(k + 1)
+                normalise(k + 1)
+            if valid(k - 1):
+                quantise_v(k - 1)
+            if valid(k):
+                quantise_p(k)

@@ -24,6 +24,7 @@ FLOPS = 2 * R * C * E * E + 2 * H * C * C * R * D
 def tile_rowselfattention_pb_kernel(tc, attn_weights, mask0, x, Wv, bv, out):
     nc = tc.nc
     with ExitStack() as ctx:
+        ctx.enter_context(tc.manual_schedule())
         keep_pool = ctx.enter_context(tc.tile_pool(name="keep", bufs=1))
         work = ctx.enter_context(tc.tile_pool(name="work", bufs=2))
         stats = ctx.enter_context(tc.tile_pool(name="stats", bufs=8))
@@ -274,26 +275,25 @@ def tile_rowselfattention_pb_kernel(tc, attn_weights, mask0, x, Wv, bv, out):
             if valid(k + 2):
                 for h0, h1 in pieces(k + 2):
                     row_max(k + 2, h0, h1)
-            if k == -2:
-                prepare_weights()
-            if valid(k + 1):
-                exponentials(k + 1)
+            if valid(k - 1):
+                quantise_p(k - 1)
+                for h in range(H):
+                    project_head(k - 1, h)
             if valid(k):
                 quantise_x(k)
-            ready = [
-                (it, r) for it in range(TILES) for r in range(R) if max(it + 1, r + 2) == k
-            ]
-            for h in range(H):
-                if valid(k - 1):
-                    project_head(k - 1, h)
-                if valid(k):
+            if valid(k + 1):
+                exponentials(k + 1)
+            if k == -1:
+                prepare_weights()
+            if valid(k):
+                for h in range(H):
                     transpose_p_head(k, h)
-                for it, r in ready[h::H]:
-                    attend(it, r)
             if valid(k + 1):
                 transpose_x(k + 1)
                 normalise(k + 1)
+            for it in range(TILES):
+                for r in range(R):
+                    if max(it + 1, r + 2) == k:
+                        attend(it, r)
             if valid(k - 1):
                 quantise_v(k - 1)
-            if valid(k):
-                quantise_p(k)

@@ -17,6 +17,7 @@ PACK = 4
 R, C, E, H = 4, 512, 512, 4
 D = E // H
 TILES = C // P
+HALVINGS = 3
 
 FLOPS = 2 * R * C * E * E + 2 * H * C * C * R * D
 
@@ -28,7 +29,7 @@ def tile_rowselfattention_pb_kernel(tc, attn_weights, mask0, x, Wv, bv, out):
         keep_pool = ctx.enter_context(tc.tile_pool(name="keep", bufs=1))
         work = ctx.enter_context(tc.tile_pool(name="work", bufs=2))
         stats = ctx.enter_context(tc.tile_pool(name="stats", bufs=8))
-        stores = ctx.enter_context(tc.tile_pool(name="stores", bufs=6))
+        stores = ctx.enter_context(tc.tile_pool(name="stores", bufs=TILES * R))
         psum = ctx.enter_context(tc.psum_pool(name="psum", bufs=8))
 
         mask_col = keep_pool.tile([P, TILES], BF16, name="mask_col")
@@ -95,12 +96,17 @@ def tile_rowselfattention_pb_kernel(tc, attn_weights, mask0, x, Wv, bv, out):
         w_codes = keep_pool.tile([P, E], U32, name="w_codes", align_bytes=64)
         w_scales = keep_pool.tile([P, E], U8, name="w_scales", align_bytes=64)
 
-        def prepare_weights():
+        w_grouped = keep_pool.tile([P, E, PACK], BF16, name="w_grouped", align_bytes=64)
+
+        def broadcast_bias():
             bias_ps = psum.tile([P, E], F32, tag="bank")
             nc.tensor.matmul(out=bias_ps[:], lhsT=ones[:], rhs=bias_row[:], start=True, stop=True)
             nc.vector.tensor_copy(out=bias_bc[:], in_=bias_ps[:])
-            w_grouped = keep_pool.tile([P, E, PACK], BF16, name="w_grouped", align_bytes=64)
+
+        def group_weights():
             nc.vector.tensor_copy(out=w_grouped[:], in_=w_raw[:].rearrange("q t c -> q c t"))
+
+        def quantise_weights():
             nc.vector.quantize_mx(
                 out=w_codes[:].bitcast(FP8X4),
                 scales=w_scales[:],
@@ -123,9 +129,12 @@ def tile_rowselfattention_pb_kernel(tc, attn_weights, mask0, x, Wv, bv, out):
 
         x_grouped = {}
         v_grouped = {}
+        rows = {}
+        logit_max = {}
         shift = {}
         e = {}
         row_sum = {}
+        inv_sum = {}
         p_bf = {}
         p_grouped = {}
 
@@ -183,32 +192,31 @@ def tile_rowselfattention_pb_kernel(tc, attn_weights, mask0, x, Wv, bv, out):
                 in_=v_grouped[r][:].rearrange("p h d t -> p (h d t)"),
             )
 
-        def row_max(it, h0, h1):
-            a = a_sb[it][:, h0:h1, :]
+        def row_max_step(it, h0, h1, halvings, step):
             heads = h1 - h0
-            half_a = work.tile([P, heads, C // 2], BF16, name="half_a")
-            nc.vector.tensor_tensor(
-                out=half_a[:], in0=a[:, :, 0 : C // 2], in1=a[:, :, C // 2 : C], op=ALU.max
-            )
-            half_b = work.tile([P, heads, C // 4], BF16, name="half_b")
-            nc.vector.tensor_tensor(
-                out=half_b[:], in0=half_a[:, :, 0 : C // 4], in1=half_a[:, :, C // 4 : C // 2],
-                op=ALU.max,
-            )
-            half_c = work.tile([P, heads, C // 8], BF16, name="half_c")
-            nc.vector.tensor_tensor(
-                out=half_c[:], in0=half_b[:, :, 0 : C // 8], in1=half_b[:, :, C // 8 : C // 4],
-                op=ALU.max,
-            )
-            logit_max = stats.tile([P, heads], F32, name="logit_max")
-            nc.vector.tensor_reduce(out=logit_max[:], in_=half_c[:], axis=AXIS.X, op=ALU.max)
-            shifts = stats.tile([P, heads], F32, name="shifts")
-            nc.vector.tensor_scalar(
-                out=shifts[:], in0=logit_max[:], scalar1=neg_keep[:, it : it + 1], scalar2=None,
-                op0=ALU.mult,
-            )
-            for h in range(h0, h1):
-                shift[(it, h)] = shifts[:, h - h0 : h - h0 + 1]
+            if step == 0:
+                rows[(it, h0, 0)] = a_sb[it][:, h0:h1, :]
+            if step < halvings:
+                src = rows[(it, h0, step)]
+                width = C >> (step + 1)
+                dst = work.tile([P, heads, width], BF16, name="half%d" % step)
+                nc.vector.tensor_tensor(
+                    out=dst[:], in0=src[:, :, 0:width], in1=src[:, :, width : 2 * width], op=ALU.max
+                )
+                rows[(it, h0, step + 1)] = dst
+            elif step == halvings:
+                logit_max[(it, h0)] = stats.tile([P, heads], F32, name="logit_max")
+                nc.vector.tensor_reduce(
+                    out=logit_max[(it, h0)][:], in_=rows[(it, h0, step)], axis=AXIS.X, op=ALU.max
+                )
+            else:
+                shifts = stats.tile([P, heads], F32, name="shifts")
+                nc.vector.tensor_scalar(
+                    out=shifts[:], in0=logit_max[(it, h0)][:], scalar1=neg_keep[:, it : it + 1],
+                    scalar2=None, op0=ALU.mult,
+                )
+                for h in range(h0, h1):
+                    shift[(it, h)] = shifts[:, h - h0 : h - h0 + 1]
 
         def exponentials(it):
             e[it] = work.tile([P, H, C], F32, name="e")
@@ -220,15 +228,16 @@ def tile_rowselfattention_pb_kernel(tc, attn_weights, mask0, x, Wv, bv, out):
                     accum_out=row_sum[it][:, h : h + 1],
                 )
 
-        def normalise(it):
-            inv_sum = stats.tile([P, H], F32, name="inv_sum")
-            nc.vector.reciprocal(out=inv_sum[:], in_=row_sum[it][:])
+        def invert_sums(it):
+            inv_sum[it] = stats.tile([P, H], F32, name="inv_sum")
+            nc.vector.reciprocal(out=inv_sum[it][:], in_=row_sum[it][:])
             p_bf[it] = work.tile([P, H, C], BF16, name="p_bf")
-            for h in range(H):
-                nc.vector.tensor_scalar(
-                    out=p_bf[it][:, h, :], in0=e[it][:, h, :], scalar1=inv_sum[:, h : h + 1],
-                    scalar2=None, op0=ALU.mult,
-                )
+
+        def normalise_head(it, h):
+            nc.vector.tensor_scalar(
+                out=p_bf[it][:, h, :], in0=e[it][:, h, :], scalar1=inv_sum[it][:, h : h + 1],
+                scalar2=None, op0=ALU.mult,
+            )
 
         def transpose_p_head(it, h):
             if h == 0:
@@ -271,29 +280,41 @@ def tile_rowselfattention_pb_kernel(tc, attn_weights, mask0, x, Wv, bv, out):
         def valid(n):
             return 0 <= n < TILES
 
-        for k in range(-2, TILES + 2):
-            if valid(k + 2):
-                for h0, h1 in pieces(k + 2):
-                    row_max(k + 2, h0, h1)
+        for h in range(H + 1):
+            if h < H:
+                row_max_step(0, h, h + 1, 0, 0)
+            if h > 0:
+                row_max_step(0, h - 1, h, 0, 1)
+        weight_steps = [broadcast_bias, group_weights, quantise_weights]
+        for step in range(HALVINGS + 2):
+            row_max_step(1, 0, H, HALVINGS, step)
+            if step < len(weight_steps):
+                weight_steps[step]()
+
+        for k in range(-1, TILES + 2):
             if valid(k - 1):
                 quantise_p(k - 1)
                 for h in range(H):
                     project_head(k - 1, h)
+            if valid(k + 1):
+                exponentials(k + 1)
             if valid(k):
                 quantise_x(k)
             if valid(k + 1):
-                exponentials(k + 1)
-            if k == -1:
-                prepare_weights()
+                invert_sums(k + 1)
             if valid(k):
                 for h in range(H):
                     transpose_p_head(k, h)
             if valid(k + 1):
                 transpose_x(k + 1)
-                normalise(k + 1)
             for it in range(TILES):
                 for r in range(R):
                     if max(it + 1, r + 2) == k:
                         attend(it, r)
             if valid(k - 1):
                 quantise_v(k - 1)
+            for step in range(HALVINGS + 2):
+                if valid(k + 3):
+                    row_max_step(k + 3, 0, H, HALVINGS, step)
+                if step < H and valid(k + 1):
+                    normalise_head(k + 1, step)

@@ -54,7 +54,10 @@ def tile_rowselfattention_pb_kernel(tc, attn_weights, mask0, x, Wv, bv, out):
                 )
 
         def load_x(r):
-            nc.sync.dma_start(out=x_sb[r][:], in_=x[r].rearrange("(t p) k -> p t k", p=P))
+            nc.sync.dma_start(
+                out=x_sb[r][:].rearrange("p (u e) k -> p u e k", u=2),
+                in_=x[r].rearrange("(u p e) k -> p u e k", u=2, e=2),
+            )
 
         with nc.allow_non_contiguous_dma(reason="512 mask values, one query column to a partition"):
             nc.sync.dma_start(out=mask_col[:], in_=mask0.rearrange("(t p) -> p t", p=P))
@@ -76,8 +79,6 @@ def tile_rowselfattention_pb_kernel(tc, attn_weights, mask0, x, Wv, bv, out):
         nc.vector.memset(warm_in[:], 0.0)
         nc.scalar.activation(out=warm_out[:], in_=warm_in[:], func=ACT.Exp)
 
-        ident_bf = keep_pool.tile([P, P], BF16, name="ident_bf")
-        make_identity(nc, ident_bf[:])
         ident_f32 = keep_pool.tile([P, P], F32, name="ident_f32")
         make_identity(nc, ident_f32[:])
         ones = keep_pool.tile([P, P], BF16, name="ones")
@@ -239,16 +240,22 @@ def tile_rowselfattention_pb_kernel(tc, attn_weights, mask0, x, Wv, bv, out):
                 scalar2=None, op0=ALU.mult,
             )
 
-        def transpose_p_head(it, h):
-            if h == 0:
+        def transpose_p_heads(it, h0):
+            if h0 == 0:
                 p_grouped[it] = work.tile([P, H, P, PACK], BF16, name="p_grouped", align_bytes=64)
-            pt_ps = psum.tile([P, PACK, P], BF16, tag="bank")
-            for t in range(PACK):
-                nc.tensor.transpose(
-                    pt_ps[:, t, :], p_bf[it][:, h, t * P : (t + 1) * P], ident_bf[:]
-                )
+            pt_ps = psum.tile([P, 2, 2, P], F32, tag="bank")
+            for g in range(2):
+                words = p_bf[it][:, h0 + g, :].bitcast(F32)
+                for u in range(2):
+                    nc.tensor.transpose(
+                        pt_ps[:, g, u, :], words[:, u * P : (u + 1) * P], ident_f32[:]
+                    )
+            grouped_words = (
+                p_grouped[it][:].rearrange("p h i t -> p (h i t)").bitcast(F32)
+                .rearrange("p (h i u) -> p h i u", h=H, u=2)
+            )
             nc.scalar.copy(
-                out=p_grouped[it][:, h, :, :], in_=pt_ps[:].rearrange("p t i -> p i t")
+                out=grouped_words[:, h0 : h0 + 2, :, :], in_=pt_ps[:].rearrange("p g u i -> p g i u")
             )
 
         def quantise_p(it):
@@ -303,8 +310,8 @@ def tile_rowselfattention_pb_kernel(tc, attn_weights, mask0, x, Wv, bv, out):
             if valid(k + 1):
                 invert_sums(k + 1)
             if valid(k):
-                for h in range(H):
-                    transpose_p_head(k, h)
+                for h0 in range(0, H, 2):
+                    transpose_p_heads(k, h0)
             if valid(k + 1):
                 transpose_x(k + 1)
             for it in range(TILES):

@@ -30,7 +30,8 @@ def tile_rowselfattention_pb_kernel(tc, attn_weights, mask0, x, Wv, bv, out):
         work = ctx.enter_context(tc.tile_pool(name="work", bufs=2))
         stats = ctx.enter_context(tc.tile_pool(name="stats", bufs=8))
         stores = ctx.enter_context(tc.tile_pool(name="stores", bufs=TILES * R))
-        psum = ctx.enter_context(tc.psum_pool(name="psum", bufs=8))
+        psum = ctx.enter_context(tc.psum_pool(name="psum", bufs=7))
+        warm_pool = ctx.enter_context(tc.psum_pool(name="warm", bufs=1))
 
         mask_col = keep_pool.tile([P, TILES], BF16, name="mask_col")
         bias_row = keep_pool.tile([P, E], BF16, name="bias_row")
@@ -98,6 +99,12 @@ def tile_rowselfattention_pb_kernel(tc, attn_weights, mask0, x, Wv, bv, out):
         w_scales = keep_pool.tile([P, E], U8, name="w_scales", align_bytes=64)
 
         w_grouped = keep_pool.tile([P, E, PACK], BF16, name="w_grouped", align_bytes=64)
+
+        warm_ps = warm_pool.tile([P, P], F32, name="warm_ps")
+
+        def keep_warm(times):
+            for i in range(times):
+                nc.tensor.matmul(out=warm_ps[:], lhsT=ident_f32[:], rhs=ident_f32[:], start=True, stop=True)
 
         def broadcast_bias():
             bias_ps = psum.tile([P, E], F32, tag="bank")
@@ -287,6 +294,7 @@ def tile_rowselfattention_pb_kernel(tc, attn_weights, mask0, x, Wv, bv, out):
         def valid(n):
             return 0 <= n < TILES
 
+        keep_warm(9)
         for h in range(H + 1):
             if h < H:
                 row_max_step(0, h, h + 1, 0, 0)
@@ -311,9 +319,12 @@ def tile_rowselfattention_pb_kernel(tc, attn_weights, mask0, x, Wv, bv, out):
                 invert_sums(k + 1)
             if valid(k):
                 for h0 in range(0, H, 2):
+                    keep_warm(2)
                     transpose_p_heads(k, h0)
             if valid(k + 1):
+                keep_warm(1)
                 transpose_x(k + 1)
+                keep_warm(1)
             for it in range(TILES):
                 for r in range(R):
                     if max(it + 1, r + 2) == k:

@@ -193,11 +193,11 @@ def tile_rowselfattention_pb_kernel(tc, attn_weights, mask0, x, Wv, bv, out):
                 op=ALU.add,
             )
 
-        def quantise_v(r):
+        def quantise_v(r, h0, h1):
             nc.vector.quantize_mx(
-                out=v_codes[r][:].bitcast(FP8X4),
-                scales=v_scales[r][:],
-                in_=v_grouped[r][:].rearrange("p h d t -> p (h d t)"),
+                out=v_codes[r][:, h0 * D : h1 * D].bitcast(FP8X4),
+                scales=v_scales[r][:, h0 * D : h1 * D],
+                in_=v_grouped[r][:, h0:h1, :, :].rearrange("p h d t -> p (h d t)"),
             )
 
         def row_max_step(it, h0, h1, halvings, step):
@@ -272,24 +272,27 @@ def tile_rowselfattention_pb_kernel(tc, attn_weights, mask0, x, Wv, bv, out):
                 in_=p_grouped[it][:].rearrange("p h i t -> p (h i t)"),
             )
 
-        def attend(it, r):
-            o_ps = psum.tile([P, H, D], F32, tag="bank")
-            for h in range(H):
-                nc.tensor.matmul_mx(
-                    out=o_ps[:, h, :],
-                    lhsT=p_codes[it][:, h * P : (h + 1) * P].bitcast(FP8X4),
-                    lhsT_scale=p_scales[it][:, h * P : (h + 1) * P],
-                    rhs=v_codes[r][:, h * D : (h + 1) * D].bitcast(FP8X4),
-                    rhs_scale=v_scales[r][:, h * D : (h + 1) * D],
-                    start=True,
-                    stop=True,
-                )
-            o_sb = stores.tile([P, E], F32, name="o_sb")
-            if r == R - 1:
-                nc.vector.tensor_copy(out=o_sb[:], in_=o_ps[:].rearrange("p h d -> p (h d)"))
-            else:
-                nc.scalar.copy(out=o_sb[:], in_=o_ps[:].rearrange("p h d -> p (h d)"))
-            nc.sync.dma_start(out=out[r, it * P : (it + 1) * P, :], in_=o_sb[:])
+        def attend(tiles, heads, r, engine):
+            o_ps = psum.tile([P, len(tiles), len(heads), D], F32, tag="bank")
+            for i, it in enumerate(tiles):
+                for j, h in enumerate(heads):
+                    nc.tensor.matmul_mx(
+                        out=o_ps[:, i, j, :],
+                        lhsT=p_codes[it][:, h * P : (h + 1) * P].bitcast(FP8X4),
+                        lhsT_scale=p_scales[it][:, h * P : (h + 1) * P],
+                        rhs=v_codes[r][:, h * D : (h + 1) * D].bitcast(FP8X4),
+                        rhs_scale=v_scales[r][:, h * D : (h + 1) * D],
+                        start=True,
+                        stop=True,
+                    )
+            o_sb = stores.tile([P, len(tiles), len(heads) * D], F32, name="o_sb")
+            engine(out=o_sb[:], in_=o_ps[:].rearrange("p i h d -> p i (h d)"))
+            nc.sync.dma_start(
+                out=out[r].rearrange("(t p) f -> p t f", p=P)[
+                    :, tiles[0] : tiles[-1] + 1, heads[0] * D : (heads[-1] + 1) * D
+                ],
+                in_=o_sb[:],
+            )
 
         def valid(n):
             return 0 <= n < TILES
@@ -306,13 +309,25 @@ def tile_rowselfattention_pb_kernel(tc, attn_weights, mask0, x, Wv, bv, out):
             if step < len(weight_steps):
                 weight_steps[step]()
 
-        for k in range(-1, TILES + 2):
+        every_head = range(H)
+        for k in range(-1, TILES + 1):
             if valid(k - 1):
                 quantise_p(k - 1)
-                for h in range(H):
-                    project_head(k - 1, h)
             if valid(k + 1):
                 exponentials(k + 1)
+                keep_warm(1)
+                transpose_x(k + 1)
+                keep_warm(1)
+            ready = sorted(
+                [(it + 1 == k, r, it) for it in range(TILES) for r in range(R) if max(it + 1, r + 2) == k]
+            )
+            for h in range(H):
+                if valid(k - 1):
+                    project_head(k - 1, h)
+                if k == TILES and h == 2:
+                    quantise_v(R - 1, 0, 2)
+                for late, r, it in ready[h * len(ready) // H : (h + 1) * len(ready) // H]:
+                    attend([it], every_head, r, nc.scalar.copy)
             if valid(k):
                 quantise_x(k)
             if valid(k + 1):
@@ -321,18 +336,17 @@ def tile_rowselfattention_pb_kernel(tc, attn_weights, mask0, x, Wv, bv, out):
                 for h0 in range(0, H, 2):
                     keep_warm(2)
                     transpose_p_heads(k, h0)
-            if valid(k + 1):
-                keep_warm(1)
-                transpose_x(k + 1)
-                keep_warm(1)
-            for it in range(TILES):
-                for r in range(R):
-                    if max(it + 1, r + 2) == k:
-                        attend(it, r)
             if valid(k - 1):
-                quantise_v(k - 1)
+                if k < TILES:
+                    quantise_v(k - 1, 0, H)
+                else:
+                    quantise_v(R - 1, 2, H)
             for step in range(HALVINGS + 2):
                 if valid(k + 3):
                     row_max_step(k + 3, 0, H, HALVINGS, step)
                 if step < H and valid(k + 1):
                     normalise_head(k + 1, step)
+        for h0 in range(0, H, 2):
+            for it in range(0, TILES, 2):
+                last = h0 > 0 and it > 0
+                attend([it, it + 1], range(h0, h0 + 2), R - 1, nc.vector.tensor_copy if last else nc.scalar.copy)

@@ -10,14 +10,12 @@ U8 = mybir.dt.uint8
 FP8X4 = mybir.dt.float8_e4m3fn_x4
 ALU = mybir.AluOpType
 ACT = mybir.ActivationFunctionType
-AXIS = mybir.AxisListType
 
 P = 128
 PACK = 4
 R, C, E, H = 4, 512, 512, 4
 D = E // H
 TILES = C // P
-HALVINGS = 3
 
 FLOPS = 2 * R * C * E * E + 2 * H * C * C * R * D
 
@@ -28,7 +26,7 @@ def tile_rowselfattention_pb_kernel(tc, attn_weights, mask0, x, Wv, bv, out):
         ctx.enter_context(tc.manual_schedule())
         keep_pool = ctx.enter_context(tc.tile_pool(name="keep", bufs=1))
         work = ctx.enter_context(tc.tile_pool(name="work", bufs=2))
-        stats = ctx.enter_context(tc.tile_pool(name="stats", bufs=8))
+        stats = ctx.enter_context(tc.tile_pool(name="stats", bufs=16))
         stores = ctx.enter_context(tc.tile_pool(name="stores", bufs=TILES * R))
         psum = ctx.enter_context(tc.psum_pool(name="psum", bufs=7))
         warm_pool = ctx.enter_context(tc.psum_pool(name="warm", bufs=1))
@@ -63,17 +61,18 @@ def tile_rowselfattention_pb_kernel(tc, attn_weights, mask0, x, Wv, bv, out):
         with nc.allow_non_contiguous_dma(reason="512 mask values, one query column to a partition"):
             nc.sync.dma_start(out=mask_col[:], in_=mask0.rearrange("(t p) -> p t", p=P))
         load_logits(0)
+        nc.sync.dma_start(out=bias_row[0:1, :], in_=bv.rearrange("(o e) -> o e", o=1))
         load_logits(1)
         nc.sync.dma_start(
             out=w_raw[:].rearrange("q (u e) c -> q u e c", u=2),
             in_=Wv.rearrange("(u q e) c -> q u e c", u=2, e=2),
         )
-        nc.sync.dma_start(out=bias_row[0:1, :], in_=bv.rearrange("(o e) -> o e", o=1))
         load_x(0)
+        load_logits(2)
         load_x(1)
-        for n in range(2, R):
-            load_logits(n)
-            load_x(n)
+        load_logits(3)
+        load_x(2)
+        load_x(3)
 
         warm_in = keep_pool.tile([P, 1], F32, name="warm_in")
         warm_out = keep_pool.tile([P, 1], F32, name="warm_out")
@@ -109,7 +108,7 @@ def tile_rowselfattention_pb_kernel(tc, attn_weights, mask0, x, Wv, bv, out):
         def broadcast_bias():
             bias_ps = psum.tile([P, E], F32, tag="bank")
             nc.tensor.matmul(out=bias_ps[:], lhsT=ones[:], rhs=bias_row[:], start=True, stop=True)
-            nc.vector.tensor_copy(out=bias_bc[:], in_=bias_ps[:])
+            nc.scalar.copy(out=bias_bc[:], in_=bias_ps[:])
 
         def group_weights():
             nc.vector.tensor_copy(out=w_grouped[:], in_=w_raw[:].rearrange("q t c -> q c t"))
@@ -137,8 +136,6 @@ def tile_rowselfattention_pb_kernel(tc, attn_weights, mask0, x, Wv, bv, out):
 
         x_grouped = {}
         v_grouped = {}
-        rows = {}
-        logit_max = {}
         shift = {}
         e = {}
         row_sum = {}
@@ -200,31 +197,14 @@ def tile_rowselfattention_pb_kernel(tc, attn_weights, mask0, x, Wv, bv, out):
                 in_=v_grouped[r][:, h0:h1, :, :].rearrange("p h d t -> p (h d t)"),
             )
 
-        def row_max_step(it, h0, h1, halvings, step):
-            heads = h1 - h0
-            if step == 0:
-                rows[(it, h0, 0)] = a_sb[it][:, h0:h1, :]
-            if step < halvings:
-                src = rows[(it, h0, step)]
-                width = C >> (step + 1)
-                dst = work.tile([P, heads, width], BF16, name="half%d" % step)
-                nc.vector.tensor_tensor(
-                    out=dst[:], in0=src[:, :, 0:width], in1=src[:, :, width : 2 * width], op=ALU.max
-                )
-                rows[(it, h0, step + 1)] = dst
-            elif step == halvings:
-                logit_max[(it, h0)] = stats.tile([P, heads], F32, name="logit_max")
-                nc.vector.tensor_reduce(
-                    out=logit_max[(it, h0)][:], in_=rows[(it, h0, step)], axis=AXIS.X, op=ALU.max
-                )
-            else:
-                shifts = stats.tile([P, heads], F32, name="shifts")
-                nc.vector.tensor_scalar(
-                    out=shifts[:], in0=logit_max[(it, h0)][:], scalar1=neg_keep[:, it : it + 1],
-                    scalar2=None, op0=ALU.mult,
-                )
-                for h in range(h0, h1):
-                    shift[(it, h)] = shifts[:, h - h0 : h - h0 + 1]
+        def scaled_max(it, h):
+            scratch = work.tile([P, C], BF16, name="scratch")
+            found = stats.tile([P, 1], F32, name="found")
+            nc.vector.tensor_scalar(
+                out=scratch[:], in0=a_sb[it][:, h, :], scalar1=neg_keep[:, it : it + 1], scalar2=None,
+                op0=ALU.mult, op1=ALU.min, accum_out=found[:],
+            )
+            shift[(it, h)] = found[:]
 
         def exponentials(it):
             e[it] = work.tile([P, H, C], F32, name="e")
@@ -297,17 +277,11 @@ def tile_rowselfattention_pb_kernel(tc, attn_weights, mask0, x, Wv, bv, out):
         def valid(n):
             return 0 <= n < TILES
 
-        keep_warm(9)
-        for h in range(H + 1):
-            if h < H:
-                row_max_step(0, h, h + 1, 0, 0)
-            if h > 0:
-                row_max_step(0, h - 1, h, 0, 1)
-        weight_steps = [broadcast_bias, group_weights, quantise_weights]
-        for step in range(HALVINGS + 2):
-            row_max_step(1, 0, H, HALVINGS, step)
-            if step < len(weight_steps):
-                weight_steps[step]()
+        keep_warm(7)
+        for h in range(H):
+            scaled_max(0, h)
+        for h in range(H):
+            scaled_max(1, h)
 
         every_head = range(H)
         for k in range(-1, TILES + 1):
@@ -315,6 +289,8 @@ def tile_rowselfattention_pb_kernel(tc, attn_weights, mask0, x, Wv, bv, out):
                 quantise_p(k - 1)
             if valid(k + 1):
                 exponentials(k + 1)
+                if k == -1:
+                    broadcast_bias()
                 keep_warm(1)
                 transpose_x(k + 1)
                 keep_warm(1)
@@ -341,11 +317,18 @@ def tile_rowselfattention_pb_kernel(tc, attn_weights, mask0, x, Wv, bv, out):
                     quantise_v(k - 1, 0, H)
                 else:
                     quantise_v(R - 1, 2, H)
-            for step in range(HALVINGS + 2):
-                if valid(k + 3):
-                    row_max_step(k + 3, 0, H, HALVINGS, step)
-                if step < H and valid(k + 1):
-                    normalise_head(k + 1, step)
+            if k < 0:
+                for h in range(H):
+                    normalise_head(0, h)
+                group_weights()
+                for h in range(H):
+                    scaled_max(2, h)
+                quantise_weights()
+            for h in range(H):
+                if k >= 0 and valid(k + 3):
+                    scaled_max(k + 3, h)
+                if k >= 0 and valid(k + 1):
+                    normalise_head(k + 1, h)
         for h0 in range(0, H, 2):
             for it in range(0, TILES, 2):
                 last = h0 > 0 and it > 0

@@ -46,10 +46,11 @@ def tile_rowselfattention_pb_kernel(tc, attn_weights, mask0, x, Wv, bv, out):
             return [(h0, h0 + step) for h0 in range(0, H, step)]
 
         def load_logits(it):
+            queries = attn_weights.rearrange("h (p t) j -> p t h j", t=TILES)
             for h0, h1 in pieces(it):
                 nc.sync.dma_start(
                     out=a_sb[it][:, h0:h1, :],
-                    in_=attn_weights[h0:h1, it * P : (it + 1) * P, :].rearrange("h p j -> p h j"),
+                    in_=queries[:, it, h0:h1, :],
                 )
 
         def load_x(r):
@@ -58,8 +59,8 @@ def tile_rowselfattention_pb_kernel(tc, attn_weights, mask0, x, Wv, bv, out):
                 in_=x[r].rearrange("(u p e) k -> p u e k", u=2, e=2),
             )
 
-        with nc.allow_non_contiguous_dma(reason="512 mask values, one query column to a partition"):
-            nc.sync.dma_start(out=mask_col[:], in_=mask0.rearrange("(t p) -> p t", p=P))
+        with nc.allow_non_contiguous_dma(reason="512 mask values, four query columns to a partition"):
+            nc.sync.dma_start(out=mask_col[:], in_=mask0.rearrange("(p t) -> p t", t=TILES))
         load_logits(0)
         nc.sync.dma_start(out=bias_row[0:1, :], in_=bv.rearrange("(o e) -> o e", o=1))
         load_logits(1)
@@ -110,8 +111,8 @@ def tile_rowselfattention_pb_kernel(tc, attn_weights, mask0, x, Wv, bv, out):
             nc.tensor.matmul(out=bias_ps[:], lhsT=ones[:], rhs=bias_row[:], start=True, stop=True)
             nc.scalar.copy(out=bias_bc[:], in_=bias_ps[:])
 
-        def group_weights():
-            nc.vector.tensor_copy(out=w_grouped[:], in_=w_raw[:].rearrange("q t c -> q c t"))
+        def group_weights(c0, c1, copy):
+            copy(out=w_grouped[:, c0:c1, :], in_=w_raw[:, :, c0:c1].rearrange("q t c -> q c t"))
 
         def quantise_weights():
             nc.vector.quantize_mx(
@@ -268,7 +269,7 @@ def tile_rowselfattention_pb_kernel(tc, attn_weights, mask0, x, Wv, bv, out):
             o_sb = stores.tile([P, len(tiles), len(heads) * D], F32, name="o_sb")
             engine(out=o_sb[:], in_=o_ps[:].rearrange("p i h d -> p i (h d)"))
             nc.sync.dma_start(
-                out=out[r].rearrange("(t p) f -> p t f", p=P)[
+                out=out[r].rearrange("(p t) f -> p t f", t=TILES)[
                     :, tiles[0] : tiles[-1] + 1, heads[0] * D : (heads[-1] + 1) * D
                 ],
                 in_=o_sb[:],
@@ -288,9 +289,12 @@ def tile_rowselfattention_pb_kernel(tc, attn_weights, mask0, x, Wv, bv, out):
             if valid(k - 1):
                 quantise_p(k - 1)
             if valid(k + 1):
-                exponentials(k + 1)
+                if k != 0:
+                    exponentials(k + 1)
                 if k == -1:
                     broadcast_bias()
+                    group_weights(0, 128, nc.scalar.copy)
+                    exponentials(1)
                 keep_warm(1)
                 transpose_x(k + 1)
                 keep_warm(1)
@@ -306,7 +310,7 @@ def tile_rowselfattention_pb_kernel(tc, attn_weights, mask0, x, Wv, bv, out):
                     attend([it], every_head, r, nc.scalar.copy)
             if valid(k):
                 quantise_x(k)
-            if valid(k + 1):
+            if valid(k + 1) and k != 0:
                 invert_sums(k + 1)
             if valid(k):
                 for h0 in range(0, H, 2):
@@ -318,16 +322,19 @@ def tile_rowselfattention_pb_kernel(tc, attn_weights, mask0, x, Wv, bv, out):
                 else:
                     quantise_v(R - 1, 2, H)
             if k < 0:
+                group_weights(128, E, nc.vector.tensor_copy)
                 for h in range(H):
                     normalise_head(0, h)
-                group_weights()
                 for h in range(H):
                     scaled_max(2, h)
                 quantise_weights()
+                invert_sums(1)
+                for h in range(H):
+                    normalise_head(1, h)
             for h in range(H):
                 if k >= 0 and valid(k + 3):
                     scaled_max(k + 3, h)
-                if k >= 0 and valid(k + 1):
+                if k > 0 and valid(k + 1):
                     normalise_head(k + 1, h)
         for h0 in range(0, H, 2):
             for it in range(0, TILES, 2):

@@ -42,7 +42,7 @@ def tile_rowselfattention_pb_kernel(tc, attn_weights, mask0, x, Wv, bv, out):
             a_sb.append(keep_pool.tile([P, H, C], BF16, name="a_sb%d" % n))
 
         def pieces(it):
-            step = 1 if it == 0 else H
+            step = [1, H // 2, H, H][it]
             return [(h0, h0 + step) for h0 in range(0, H, step)]
 
         def load_logits(it):
@@ -109,7 +109,7 @@ def tile_rowselfattention_pb_kernel(tc, attn_weights, mask0, x, Wv, bv, out):
         def broadcast_bias():
             bias_ps = psum.tile([P, E], F32, tag="bank")
             nc.tensor.matmul(out=bias_ps[:], lhsT=ones[:], rhs=bias_row[:], start=True, stop=True)
-            nc.scalar.copy(out=bias_bc[:], in_=bias_ps[:])
+            nc.vector.tensor_copy(out=bias_bc[:], in_=bias_ps[:])
 
         def group_weights(c0, c1, copy):
             copy(out=w_grouped[:, c0:c1, :], in_=w_raw[:, :, c0:c1].rearrange("q t c -> q c t"))
@@ -223,10 +223,16 @@ def tile_rowselfattention_pb_kernel(tc, attn_weights, mask0, x, Wv, bv, out):
             p_bf[it] = work.tile([P, H, C], BF16, name="p_bf")
 
         def normalise_head(it, h):
-            nc.vector.tensor_scalar(
-                out=p_bf[it][:, h, :], in0=e[it][:, h, :], scalar1=inv_sum[it][:, h : h + 1],
-                scalar2=None, op0=ALU.mult,
-            )
+            if it == TILES - 1 and h >= H - 1:
+                nc.scalar.activation(
+                    out=p_bf[it][:, h, :], in_=e[it][:, h, :], func=ACT.Copy,
+                    scale=inv_sum[it][:, h : h + 1],
+                )
+            else:
+                nc.vector.tensor_scalar(
+                    out=p_bf[it][:, h, :], in0=e[it][:, h, :], scalar1=inv_sum[it][:, h : h + 1],
+                    scalar2=None, op0=ALU.mult,
+                )
 
         def transpose_p_heads(it, h0):
             if h0 == 0:
@@ -278,57 +284,76 @@ def tile_rowselfattention_pb_kernel(tc, attn_weights, mask0, x, Wv, bv, out):
         def valid(n):
             return 0 <= n < TILES
 
-        keep_warm(7)
+        keep_warm(4)
         for h in range(H):
             scaled_max(0, h)
         for h in range(H):
             scaled_max(1, h)
+        broadcast_bias()
+        keep_warm(3)
 
         every_head = range(H)
         for k in range(-1, TILES + 1):
-            if valid(k - 1):
+            if valid(k - 1) and k < TILES:
                 quantise_p(k - 1)
             if valid(k + 1):
                 if k != 0:
                     exponentials(k + 1)
                 if k == -1:
-                    broadcast_bias()
                     group_weights(0, 128, nc.scalar.copy)
                     exponentials(1)
+                if k == 0:
+                    for h0 in range(0, H, 2):
+                        keep_warm(2)
+                        transpose_p_heads(0, h0)
                 keep_warm(1)
                 transpose_x(k + 1)
                 keep_warm(1)
             ready = sorted(
-                [(it + 1 == k, r, it) for it in range(TILES) for r in range(R) if max(it + 1, r + 2) == k]
+                [
+                    (it + 1 == k, r, it) for r in range(R) for it in range(TILES)
+                    if max(it + 1, r + 2) == k and (it < TILES - 1 or r == R - 2)
+                ]
             )
+            slots = [1, 2, 2, len(ready)] if k == TILES - 1 else [n * len(ready) // H for n in range(1, H + 1)]
+            done = 0
             for h in range(H):
                 if valid(k - 1):
                     project_head(k - 1, h)
                 if k == TILES and h == 2:
                     quantise_v(R - 1, 0, 2)
-                for late, r, it in ready[h * len(ready) // H : (h + 1) * len(ready) // H]:
+                if k == TILES - 1 and h in (1, 2):
+                    transpose_p_heads(k, 2 * (h - 1))
+                for late, r, it in ready[done : slots[h]]:
                     attend([it], every_head, r, nc.scalar.copy)
+                done = slots[h]
+            if k == TILES - 1:
+                quantise_p(k)
             if valid(k):
                 quantise_x(k)
             if valid(k + 1) and k != 0:
                 invert_sums(k + 1)
-            if valid(k):
+            if 0 < k < TILES - 1:
                 for h0 in range(0, H, 2):
-                    keep_warm(2)
+                    keep_warm(1)
                     transpose_p_heads(k, h0)
             if valid(k - 1):
                 if k < TILES:
                     quantise_v(k - 1, 0, H)
                 else:
-                    quantise_v(R - 1, 2, H)
+                    for h in range(2, H):
+                        quantise_v(R - 1, h, h + 1)
+            if k == TILES - 1:
+                for r in range(R - 2):
+                    attend([k], every_head, r, nc.scalar.copy)
             if k < 0:
                 group_weights(128, E, nc.vector.tensor_copy)
                 for h in range(H):
                     normalise_head(0, h)
                 for h in range(H):
                     scaled_max(2, h)
-                quantise_weights()
                 invert_sums(1)
+                quantise_weights()
                 for h in range(H):
                     normalise_head(1, h)
             for h in range(H):
@@ -336,7 +361,7 @@ def tile_rowselfattention_pb_kernel(tc, attn_weights, mask0, x, Wv, bv, out):
                     scaled_max(k + 3, h)
                 if k > 0 and valid(k + 1):
                     normalise_head(k + 1, h)
-        for h0 in range(0, H, 2):
-            for it in range(0, TILES, 2):
-                last = h0 > 0 and it > 0
-                attend([it, it + 1], range(h0, h0 + 2), R - 1, nc.vector.tensor_copy if last else nc.scalar.copy)
+        attend(range(0, 2), range(0, 2), R - 1, nc.scalar.copy)
+        attend(range(2, TILES), range(0, 2), R - 1, nc.vector.tensor_copy)
+        attend(range(TILES), [2], R - 1, nc.scalar.copy)
+        attend(range(TILES), [3], R - 1, nc.vector.tensor_copy)

from contextlib import ExitStack

import concourse.mybir as mybir
from concourse.masks import make_identity

F32 = mybir.dt.float32
BF16 = mybir.dt.bfloat16
U32 = mybir.dt.uint32
U8 = mybir.dt.uint8
FP8X4 = mybir.dt.float8_e4m3fn_x4
ALU = mybir.AluOpType
ACT = mybir.ActivationFunctionType

P = 128
PACK = 4
R, C, E, H = 4, 512, 512, 4
D = E // H
TILES = C // P

FLOPS = 2 * R * C * E * E + 2 * H * C * C * R * D


def tile_rowselfattention_pb_kernel(tc, attn_weights, mask0, x, Wv, bv, out):
    nc = tc.nc
    with ExitStack() as ctx:
        ctx.enter_context(tc.manual_schedule())
        keep_pool = ctx.enter_context(tc.tile_pool(name="keep", bufs=1))
        work = ctx.enter_context(tc.tile_pool(name="work", bufs=2))
        stats = ctx.enter_context(tc.tile_pool(name="stats", bufs=16))
        stores = ctx.enter_context(tc.tile_pool(name="stores", bufs=TILES * R))
        psum = ctx.enter_context(tc.psum_pool(name="psum", bufs=7))
        warm_pool = ctx.enter_context(tc.psum_pool(name="warm", bufs=1))

        mask_col = keep_pool.tile([P, TILES], BF16, name="mask_col")
        bias_row = keep_pool.tile([P, E], BF16, name="bias_row")
        nc.gpsimd.memset(bias_row[:], 0.0)
        w_raw = keep_pool.tile([P, PACK, E], BF16, name="w_raw")
        x_sb = []
        a_sb = []
        for n in range(R):
            x_sb.append(keep_pool.tile([P, TILES, E], BF16, name="x_sb%d" % n))
            a_sb.append(keep_pool.tile([P, H, C], BF16, name="a_sb%d" % n))

        def pieces(it):
            step = [1, H // 2, H, H][it]
            return [(h0, h0 + step) for h0 in range(0, H, step)]

        def load_logits(it):
            queries = attn_weights.rearrange("h (p t) j -> p t h j", t=TILES)
            for h0, h1 in pieces(it):
                nc.sync.dma_start(
                    out=a_sb[it][:, h0:h1, :],
                    in_=queries[:, it, h0:h1, :],
                )

        def load_x(r):
            nc.sync.dma_start(
                out=x_sb[r][:].rearrange("p (u e) k -> p u e k", u=2),
                in_=x[r].rearrange("(u p e) k -> p u e k", u=2, e=2),
            )

        with nc.allow_non_contiguous_dma(reason="512 mask values, four query columns to a partition"):
            nc.sync.dma_start(out=mask_col[:], in_=mask0.rearrange("(p t) -> p t", t=TILES))
        load_logits(0)
        nc.sync.dma_start(out=bias_row[0:1, :], in_=bv.rearrange("(o e) -> o e", o=1))
        load_logits(1)
        nc.sync.dma_start(
            out=w_raw[:].rearrange("q (u e) c -> q u e c", u=2),
            in_=Wv.rearrange("(u q e) c -> q u e c", u=2, e=2),
        )
        load_x(0)
        load_logits(2)
        load_x(1)
        load_logits(3)
        load_x(2)
        load_x(3)

        warm_in = keep_pool.tile([P, 1], F32, name="warm_in")
        warm_out = keep_pool.tile([P, 1], F32, name="warm_out")
        nc.vector.memset(warm_in[:], 0.0)
        nc.scalar.activation(out=warm_out[:], in_=warm_in[:], func=ACT.Exp)

        ident_f32 = keep_pool.tile([P, P], F32, name="ident_f32")
        make_identity(nc, ident_f32[:])
        ones = keep_pool.tile([P, P], BF16, name="ones")
        nc.vector.memset(ones[:], 1.0)

        keep = keep_pool.tile([P, TILES], F32, name="keep")
        nc.vector.tensor_scalar(
            out=keep[:], in0=mask_col[:], scalar1=-1.0, scalar2=1.0, op0=ALU.mult, op1=ALU.add
        )
        neg_keep = keep_pool.tile([P, TILES], F32, name="neg_keep")
        nc.vector.tensor_scalar(
            out=neg_keep[:], in0=mask_col[:], scalar1=-1.0, scalar2=None, op0=ALU.add
        )

        bias_bc = keep_pool.tile([P, E], F32, name="bias_bc")
        w_codes = keep_pool.tile([P, E], U32, name="w_codes", align_bytes=64)
        w_scales = keep_pool.tile([P, E], U8, name="w_scales", align_bytes=64)

        w_grouped = keep_pool.tile([P, E, PACK], BF16, name="w_grouped", align_bytes=64)

        warm_ps = warm_pool.tile([P, P], F32, name="warm_ps")

        def keep_warm(times):
            for i in range(times):
                nc.tensor.matmul(out=warm_ps[:], lhsT=ident_f32[:], rhs=ident_f32[:], start=True, stop=True)

        def broadcast_bias():
            bias_ps = psum.tile([P, E], F32, tag="bank")
            nc.tensor.matmul(out=bias_ps[:], lhsT=ones[:], rhs=bias_row[:], start=True, stop=True)
            nc.vector.tensor_copy(out=bias_bc[:], in_=bias_ps[:])

        def group_weights(c0, c1, copy):
            copy(out=w_grouped[:, c0:c1, :], in_=w_raw[:, :, c0:c1].rearrange("q t c -> q c t"))

        def quantise_weights():
            nc.vector.quantize_mx(
                out=w_codes[:].bitcast(FP8X4),
                scales=w_scales[:],
                in_=w_grouped[:].rearrange("q c t -> q (c t)"),
            )

        x_codes = []
        x_scales = []
        v_codes = []
        v_scales = []
        p_codes = []
        p_scales = []
        for n in range(R):
            x_codes.append(keep_pool.tile([P, C], U32, name="x_codes%d" % n, align_bytes=64))
            x_scales.append(keep_pool.tile([P, C], U8, name="x_scales%d" % n, align_bytes=64))
            v_codes.append(keep_pool.tile([P, E], U32, name="v_codes%d" % n, align_bytes=64))
            v_scales.append(keep_pool.tile([P, E], U8, name="v_scales%d" % n, align_bytes=64))
            p_codes.append(keep_pool.tile([P, H * P], U32, name="p_codes%d" % n, align_bytes=64))
            p_scales.append(keep_pool.tile([P, H * P], U8, name="p_scales%d" % n, align_bytes=64))

        x_grouped = {}
        v_grouped = {}
        shift = {}
        e = {}
        row_sum = {}
        inv_sum = {}
        p_bf = {}
        p_grouped = {}

        def transpose_x(r):
            x_grouped[r] = work.tile([P, C, PACK], BF16, name="x_grouped", align_bytes=64)
            grouped_words = (
                x_grouped[r][:].rearrange("p j t -> p (j t)").bitcast(F32)
                .rearrange("p (g j u) -> p g j u", g=TILES, u=2)
            )
            for half in range(2):
                xt_ps = psum.tile([P, 2, 2, P], F32, tag="bank")
                for g in range(2):
                    words = x_sb[r][:, 2 * half + g, :].bitcast(F32)
                    for u in range(2):
                        nc.tensor.transpose(
                            xt_ps[:, g, u, :], words[:, u * P : (u + 1) * P], ident_f32[:]
                        )
                nc.scalar.copy(
                    out=grouped_words[:, 2 * half : 2 * half + 2, :, :],
                    in_=xt_ps[:].rearrange("p g u j -> p g j u"),
                )

        def quantise_x(r):
            nc.vector.quantize_mx(
                out=x_codes[r][:].bitcast(FP8X4),
                scales=x_scales[r][:],
                in_=x_grouped[r][:].rearrange("p j t -> p (j t)"),
            )

        def project_head(r, h):
            if h == 0:
                v_grouped[r] = work.tile([P, H, D, PACK], BF16, name="v_grouped", align_bytes=64)
            v_ps = psum.tile([P, PACK, D], F32, tag="bank")
            for t in range(PACK):
                nc.tensor.matmul_mx(
                    out=v_ps[:, t, :],
                    lhsT=x_codes[r][:, t * P : (t + 1) * P].bitcast(FP8X4),
                    lhsT_scale=x_scales[r][:, t * P : (t + 1) * P],
                    rhs=w_codes[:, h * D : (h + 1) * D].bitcast(FP8X4),
                    rhs_scale=w_scales[:, h * D : (h + 1) * D],
                    start=True,
                    stop=True,
                )
            nc.vector.tensor_tensor(
                out=v_grouped[r][:, h, :, :],
                in0=v_ps[:].rearrange("p t d -> p d t"),
                in1=bias_bc[:, h * D : (h + 1) * D].unsqueeze(2).to_broadcast([P, D, PACK]),
                op=ALU.add,
            )

        def quantise_v(r, h0, h1):
            nc.vector.quantize_mx(
                out=v_codes[r][:, h0 * D : h1 * D].bitcast(FP8X4),
                scales=v_scales[r][:, h0 * D : h1 * D],
                in_=v_grouped[r][:, h0:h1, :, :].rearrange("p h d t -> p (h d t)"),
            )

        def scaled_max(it, h):
            scratch = work.tile([P, C], BF16, name="scratch")
            found = stats.tile([P, 1], F32, name="found")
            nc.vector.tensor_scalar(
                out=scratch[:], in0=a_sb[it][:, h, :], scalar1=neg_keep[:, it : it + 1], scalar2=None,
                op0=ALU.mult, op1=ALU.min, accum_out=found[:],
            )
            shift[(it, h)] = found[:]

        def exponentials(it):
            e[it] = work.tile([P, H, C], F32, name="e")
            row_sum[it] = stats.tile([P, H], F32, name="row_sum")
            for h in range(H):
                nc.scalar.activation(
                    out=e[it][:, h, :], in_=a_sb[it][:, h, :], func=ACT.Exp,
                    bias=shift[(it, h)], scale=keep[:, it : it + 1],
                    accum_out=row_sum[it][:, h : h + 1],
                )

        def invert_sums(it):
            inv_sum[it] = stats.tile([P, H], F32, name="inv_sum")
            nc.vector.reciprocal(out=inv_sum[it][:], in_=row_sum[it][:])
            p_bf[it] = work.tile([P, H, C], BF16, name="p_bf")

        def normalise_head(it, h):
            if it == TILES - 1 and h >= H - 1:
                nc.scalar.activation(
                    out=p_bf[it][:, h, :], in_=e[it][:, h, :], func=ACT.Copy,
                    scale=inv_sum[it][:, h : h + 1],
                )
            else:
                nc.vector.tensor_scalar(
                    out=p_bf[it][:, h, :], in0=e[it][:, h, :], scalar1=inv_sum[it][:, h : h + 1],
                    scalar2=None, op0=ALU.mult,
                )

        def transpose_p_heads(it, h0):
            if h0 == 0:
                p_grouped[it] = work.tile([P, H, P, PACK], BF16, name="p_grouped", align_bytes=64)
            pt_ps = psum.tile([P, 2, 2, P], F32, tag="bank")
            for g in range(2):
                words = p_bf[it][:, h0 + g, :].bitcast(F32)
                for u in range(2):
                    nc.tensor.transpose(
                        pt_ps[:, g, u, :], words[:, u * P : (u + 1) * P], ident_f32[:]
                    )
            grouped_words = (
                p_grouped[it][:].rearrange("p h i t -> p (h i t)").bitcast(F32)
                .rearrange("p (h i u) -> p h i u", h=H, u=2)
            )
            nc.scalar.copy(
                out=grouped_words[:, h0 : h0 + 2, :, :], in_=pt_ps[:].rearrange("p g u i -> p g i u")
            )

        def quantise_p(it):
            nc.vector.quantize_mx(
                out=p_codes[it][:].bitcast(FP8X4),
                scales=p_scales[it][:],
                in_=p_grouped[it][:].rearrange("p h i t -> p (h i t)"),
            )

        def attend(tiles, heads, r, engine):
            o_ps = psum.tile([P, len(tiles), len(heads), D], F32, tag="bank")
            for i, it in enumerate(tiles):
                for j, h in enumerate(heads):
                    nc.tensor.matmul_mx(
                        out=o_ps[:, i, j, :],
                        lhsT=p_codes[it][:, h * P : (h + 1) * P].bitcast(FP8X4),
                        lhsT_scale=p_scales[it][:, h * P : (h + 1) * P],
                        rhs=v_codes[r][:, h * D : (h + 1) * D].bitcast(FP8X4),
                        rhs_scale=v_scales[r][:, h * D : (h + 1) * D],
                        start=True,
                        stop=True,
                    )
            o_sb = stores.tile([P, len(tiles), len(heads) * D], F32, name="o_sb")
            engine(out=o_sb[:], in_=o_ps[:].rearrange("p i h d -> p i (h d)"))
            nc.sync.dma_start(
                out=out[r].rearrange("(p t) f -> p t f", t=TILES)[
                    :, tiles[0] : tiles[-1] + 1, heads[0] * D : (heads[-1] + 1) * D
                ],
                in_=o_sb[:],
            )

        def valid(n):
            return 0 <= n < TILES

        keep_warm(4)
        for h in range(H):
            scaled_max(0, h)
        for h in range(H):
            scaled_max(1, h)
        broadcast_bias()
        keep_warm(3)

        every_head = range(H)
        for k in range(-1, TILES + 1):
            if valid(k - 1) and k < TILES:
                quantise_p(k - 1)
            if valid(k + 1):
                if k != 0:
                    exponentials(k + 1)
                if k == -1:
                    group_weights(0, 128, nc.scalar.copy)
                    exponentials(1)
                if k == 0:
                    for h0 in range(0, H, 2):
                        keep_warm(2)
                        transpose_p_heads(0, h0)
                keep_warm(1)
                transpose_x(k + 1)
                keep_warm(1)
            ready = sorted(
                [
                    (it + 1 == k, r, it) for r in range(R) for it in range(TILES)
                    if max(it + 1, r + 2) == k and (it < TILES - 1 or r == R - 2)
                ]
            )
            slots = [1, 2, 2, len(ready)] if k == TILES - 1 else [n * len(ready) // H for n in range(1, H + 1)]
            done = 0
            for h in range(H):
                if valid(k - 1):
                    project_head(k - 1, h)
                if k == TILES and h == 2:
                    quantise_v(R - 1, 0, 2)
                if k == TILES - 1 and h in (1, 2):
                    transpose_p_heads(k, 2 * (h - 1))
                for late, r, it in ready[done : slots[h]]:
                    attend([it], every_head, r, nc.scalar.copy)
                done = slots[h]
            if k == TILES - 1:
                quantise_p(k)
            if valid(k):
                quantise_x(k)
            if valid(k + 1) and k != 0:
                invert_sums(k + 1)
            if 0 < k < TILES - 1:
                for h0 in range(0, H, 2):
                    keep_warm(1)
                    transpose_p_heads(k, h0)
            if valid(k - 1):
                if k < TILES:
                    quantise_v(k - 1, 0, H)
                else:
                    for h in range(2, H):
                        quantise_v(R - 1, h, h + 1)
            if k == TILES - 1:
                for r in range(R - 2):
                    attend([k], every_head, r, nc.scalar.copy)
            if k < 0:
                group_weights(128, E, nc.vector.tensor_copy)
                for h in range(H):
                    normalise_head(0, h)
                for h in range(H):
                    scaled_max(2, h)
                invert_sums(1)
                quantise_weights()
                for h in range(H):
                    normalise_head(1, h)
            for h in range(H):
                if k >= 0 and valid(k + 3):
                    scaled_max(k + 3, h)
                if k > 0 and valid(k + 1):
                    normalise_head(k + 1, h)
        attend(range(0, 2), range(0, 2), R - 1, nc.scalar.copy)
        attend(range(2, TILES), range(0, 2), R - 1, nc.vector.tensor_copy)
        attend(range(TILES), [2], R - 1, nc.scalar.copy)
        attend(range(TILES), [3], R - 1, nc.vector.tensor_copy)
